import numpy as np
import ml_dtypes

BF16 = ml_dtypes.bfloat16


def bf(x):
    return np.asarray(x, np.float32).astype(BF16)


def f32(x):
    return np.asarray(x, np.float32)


def f64(x):
    return np.asarray(x).astype(np.float64)


def striped(idx):
    return np.tile(idx.reshape(-1, 16).T, (8, 1))


C, S, N, HC = 1024, 512, 128, 512
THETA = 10000.0


def rotary_tables():
    th = np.float32(1.0) / np.power(np.float32(THETA), np.arange(0, C, 2, dtype=np.float32) / np.float32(C))
    fr = th[:, None] * np.arange(N, dtype=np.float32)[None, :]
    fr = np.concatenate([fr, fr], axis=0)
    return np.cos(fr), np.sin(fr)


def setup_inputs():
    cos_tab, sin_tab = rotary_tables()
    return {"emb": f32(np.random.standard_normal((C, S))), "cos_tab": f32(cos_tab), "sin_tab": f32(sin_tab), "offs": striped(np.random.permutation(np.tile(np.arange(S), 2))[:N])}


def reference(emb, cos_tab, sin_tab, offs):
    idx = offs[:16].T.reshape(-1)
    x = f64(emb)[:, idx]
    rot = np.concatenate([-x[HC:], x[:HC]], axis=0)
    return x * f64(cos_tab) + rot * f64(sin_tab)

@@ -1,0 +1,39 @@
+import concourse.mybir as mybir
+
+F32 = mybir.dt.float32
+U16 = mybir.dt.uint16
+MULT = mybir.AluOpType.mult
+ADD = mybir.AluOpType.add
+SUBTRACT = mybir.AluOpType.subtract
+
+P = 128
+C, S, N = 1024, 512, 128
+BLOCKS = C // P
+HALF = BLOCKS // 2
+
+
+def tile_sedd4rec_kernel(tc, emb, cos_tab, sin_tab, offs, out):
+    nc = tc.nc
+    with tc.tile_pool(name="held", bufs=1) as held, tc.tile_pool(name="work", bufs=4) as work:
+        offsets = held.tile([P, N // 16], U16, name="offsets")
+        nc.sync.dma_start(offsets[:], offs)
+
+        def load_block(source, b, width, label, queue):
+            block = held.tile([P, width], F32, name=f"{label}{b}")
+            queue.dma_start(block[:], source[b * P : (b + 1) * P, :])
+            return block
+
+        for lo in range(HALF):
+            hi = lo + HALF
+            window = {b: load_block(emb, b, S, "emb", nc.sync) for b in (lo, hi)}
+            cos = {b: load_block(cos_tab, b, N, "cos", nc.scalar) for b in (lo, hi)}
+            sin = {b: load_block(sin_tab, b, N, "sin", nc.scalar) for b in (lo, hi)}
+
+            for b, partner, join in ((lo, hi, SUBTRACT), (hi, lo, ADD)):
+                own = work.tile([P, N], F32, name="own")
+                nc.vector.tensor_tensor(own[:], window[b][:].indirect(offsets[:]), cos[b][:], MULT)
+                other = work.tile([P, N], F32, name="other")
+                nc.vector.tensor_tensor(other[:], window[partner][:].indirect(offsets[:]), sin[b][:], MULT)
+                rotated = work.tile([P, N], F32, name="rotated")
+                nc.vector.tensor_tensor(rotated[:], own[:], other[:], join)
+                nc.sync.dma_start(out[b * P : (b + 1) * P, :], rotated[:])

@@ -8,32 +8,39 @@ SUBTRACT = mybir.AluOpType.subtract
 
 P = 128
 C, S, N = 1024, 512, 128
-BLOCKS = C // P
-HALF = BLOCKS // 2
+HALVES = 2
+Q = C // (HALVES * P)
 
 
 def tile_sedd4rec_kernel(tc, emb, cos_tab, sin_tab, offs, out):
     nc = tc.nc
+    emb_windows = emb.rearrange("(h p q) s -> h q p s", h=HALVES, q=Q)
+    cos_halves = cos_tab.rearrange("(h p q) n -> h p q n", h=HALVES, q=Q)
+    sin_halves = sin_tab.rearrange("(h p q) n -> h p q n", h=HALVES, q=Q)
+    out_pairs = out.rearrange("(h p q) n -> q p h n", h=HALVES, q=Q)
+
     with tc.tile_pool(name="held", bufs=1) as held, tc.tile_pool(name="work", bufs=4) as work:
         offsets = held.tile([P, N // 16], U16, name="offsets")
         nc.sync.dma_start(offsets[:], offs)
 
-        def load_block(source, b, width, label, queue):
-            block = held.tile([P, width], F32, name=f"{label}{b}")
-            queue.dma_start(block[:], source[b * P : (b + 1) * P, :])
-            return block
+        cos, sin = [], []
+        for h in range(HALVES):
+            cos.append(held.tile([P, Q, N], F32, name=f"cos{h}"))
+            nc.scalar.dma_start(cos[h][:], cos_halves[h])
+            sin.append(held.tile([P, Q, N], F32, name=f"sin{h}"))
+            nc.scalar.dma_start(sin[h][:], sin_halves[h])
 
-        for lo in range(HALF):
-            hi = lo + HALF
-            window = {b: load_block(emb, b, S, "emb", nc.sync) for b in (lo, hi)}
-            cos = {b: load_block(cos_tab, b, N, "cos", nc.scalar) for b in (lo, hi)}
-            sin = {b: load_block(sin_tab, b, N, "sin", nc.scalar) for b in (lo, hi)}
+        for q in range(Q):
+            window = []
+            for h in range(HALVES):
+                window.append(held.tile([P, S], F32, name=f"emb{h}{q}"))
+                nc.sync.dma_start(window[h][:], emb_windows[h, q])
 
-            for b, partner, join in ((lo, hi, SUBTRACT), (hi, lo, ADD)):
+            rotated = work.tile([P, HALVES, N], F32, name="rotated")
+            for h, join in ((0, SUBTRACT), (1, ADD)):
                 own = work.tile([P, N], F32, name="own")
-                nc.vector.tensor_tensor(own[:], window[b][:].indirect(offsets[:]), cos[b][:], MULT)
+                nc.vector.tensor_tensor(own[:], window[h][:].indirect(offsets[:]), cos[h][:, q, :], MULT)
                 other = work.tile([P, N], F32, name="other")
-                nc.vector.tensor_tensor(other[:], window[partner][:].indirect(offsets[:]), sin[b][:], MULT)
-                rotated = work.tile([P, N], F32, name="rotated")
-                nc.vector.tensor_tensor(rotated[:], own[:], other[:], join)
-                nc.sync.dma_start(out[b * P : (b + 1) * P, :], rotated[:])
+                nc.vector.tensor_tensor(other[:], window[1 - h][:].indirect(offsets[:]), sin[h][:, q, :], MULT)
+                nc.vector.tensor_tensor(rotated[:, h, :], own[:], other[:], join)
+            nc.scalar.dma_start(out_pairs[q], rotated[:])

@@ -10,37 +10,39 @@ P = 128
 C, S, N = 1024, 512, 128
 HALVES = 2
 Q = C // (HALVES * P)
+G = 2
 
 
 def tile_sedd4rec_kernel(tc, emb, cos_tab, sin_tab, offs, out):
     nc = tc.nc
     emb_windows = emb.rearrange("(h p q) s -> h q p s", h=HALVES, q=Q)
-    cos_halves = cos_tab.rearrange("(h p q) n -> h p q n", h=HALVES, q=Q)
-    sin_halves = sin_tab.rearrange("(h p q) n -> h p q n", h=HALVES, q=Q)
+    cos_pieces = cos_tab.rearrange("(h p t g) n -> h t p g n", h=HALVES, t=Q // G, g=G)
+    sin_pieces = sin_tab.rearrange("(h p t g) n -> h t p g n", h=HALVES, t=Q // G, g=G)
     out_pairs = out.rearrange("(h p q) n -> q p h n", h=HALVES, q=Q)
 
-    with tc.tile_pool(name="held", bufs=1) as held, tc.tile_pool(name="work", bufs=4) as work:
+    with tc.tile_pool(name="held", bufs=1) as held, tc.tile_pool(name="work", bufs=3) as work:
         offsets = held.tile([P, N // 16], U16, name="offsets")
         nc.sync.dma_start(offsets[:], offs)
 
-        cos, sin = [], []
-        for h in range(HALVES):
-            cos.append(held.tile([P, Q, N], F32, name=f"cos{h}"))
-            nc.scalar.dma_start(cos[h][:], cos_halves[h])
-            sin.append(held.tile([P, Q, N], F32, name=f"sin{h}"))
-            nc.scalar.dma_start(sin[h][:], sin_halves[h])
-
+        cos = [None, None]
+        sin = [None, None]
         for q in range(Q):
-            window = []
+            t, g = divmod(q, G)
+            own = work.tile([P, HALVES, N], F32, name="own")
+            partner = work.tile([P, HALVES, N], F32, name="partner")
             for h in range(HALVES):
-                window.append(held.tile([P, S], F32, name=f"emb{h}{q}"))
-                nc.sync.dma_start(window[h][:], emb_windows[h, q])
+                window = held.tile([P, S], F32, name=f"emb{h}{q}")
+                nc.sync.dma_start(window[:], emb_windows[h, q])
+                if g == 0:
+                    cos[h] = held.tile([P, G, N], F32, name=f"cos{h}{t}")
+                    nc.sync.dma_start(cos[h][:], cos_pieces[h, t])
+                    sin[1 - h] = held.tile([P, G, N], F32, name=f"sin{1 - h}{t}")
+                    nc.sync.dma_start(sin[1 - h][:], sin_pieces[1 - h, t])
+                looked_up = window[:].indirect(offsets[:])
+                nc.vector.tensor_tensor(own[:, h, :], looked_up, cos[h][:, g, :], MULT)
+                nc.vector.tensor_tensor(partner[:, 1 - h, :], looked_up, sin[1 - h][:, g, :], MULT)
 
             rotated = work.tile([P, HALVES, N], F32, name="rotated")
-            for h, join in ((0, SUBTRACT), (1, ADD)):
-                own = work.tile([P, N], F32, name="own")
-                nc.vector.tensor_tensor(own[:], window[h][:].indirect(offsets[:]), cos[h][:, q, :], MULT)
-                other = work.tile([P, N], F32, name="other")
-                nc.vector.tensor_tensor(other[:], window[1 - h][:].indirect(offsets[:]), sin[h][:, q, :], MULT)
-                nc.vector.tensor_tensor(rotated[:, h, :], own[:], other[:], join)
+            nc.vector.tensor_tensor(rotated[:, 0, :], own[:, 0, :], partner[:, 0, :], SUBTRACT)
+            nc.vector.tensor_tensor(rotated[:, 1, :], own[:, 1, :], partner[:, 1, :], ADD)
             nc.scalar.dma_start(out_pairs[q], rotated[:])

@@ -26,6 +26,7 @@ def tile_sedd4rec_kernel(tc, emb, cos_tab, sin_tab, offs, out):
 
         cos = [None, None]
         sin = [None, None]
+        rotated = []
         for q in range(Q):
             t, g = divmod(q, G)
             own = work.tile([P, HALVES, N], F32, name="own")
@@ -42,7 +43,9 @@ def tile_sedd4rec_kernel(tc, emb, cos_tab, sin_tab, offs, out):
                 nc.vector.tensor_tensor(own[:, h, :], looked_up, cos[h][:, g, :], MULT)
                 nc.vector.tensor_tensor(partner[:, 1 - h, :], looked_up, sin[1 - h][:, g, :], MULT)
 
-            rotated = work.tile([P, HALVES, N], F32, name="rotated")
-            nc.vector.tensor_tensor(rotated[:, 0, :], own[:, 0, :], partner[:, 0, :], SUBTRACT)
-            nc.vector.tensor_tensor(rotated[:, 1, :], own[:, 1, :], partner[:, 1, :], ADD)
-            nc.scalar.dma_start(out_pairs[q], rotated[:])
+            rotated.append(held.tile([P, HALVES, N], F32, name=f"rotated{q}"))
+            nc.vector.tensor_tensor(rotated[q][:, 0, :], own[:, 0, :], partner[:, 0, :], SUBTRACT)
+            nc.vector.tensor_tensor(rotated[q][:, 1, :], own[:, 1, :], partner[:, 1, :], ADD)
+
+        for q in range(Q):
+            nc.sync.dma_start(out_pairs[q], rotated[q][:])

@@ -16,36 +16,34 @@ G = 2
 def tile_sedd4rec_kernel(tc, emb, cos_tab, sin_tab, offs, out):
     nc = tc.nc
     emb_windows = emb.rearrange("(h p q) s -> h q p s", h=HALVES, q=Q)
-    cos_pieces = cos_tab.rearrange("(h p t g) n -> h t p g n", h=HALVES, t=Q // G, g=G)
-    sin_pieces = sin_tab.rearrange("(h p t g) n -> h t p g n", h=HALVES, t=Q // G, g=G)
-    out_pairs = out.rearrange("(h p q) n -> q p h n", h=HALVES, q=Q)
+    cos_pieces = cos_tab.rearrange("(o p t g) n -> o t p g n", o=HALVES, t=Q // G, g=G)
+    sin_pieces = sin_tab.rearrange("(o p t g) n -> o t p g n", o=HALVES, t=Q // G, g=G)
+    out_pairs = out.rearrange("(o p q) n -> q p o n", o=HALVES, q=Q)
 
     with tc.tile_pool(name="held", bufs=1) as held, tc.tile_pool(name="work", bufs=3) as work:
         offsets = held.tile([P, N // 16], U16, name="offsets")
         nc.sync.dma_start(offsets[:], offs)
 
-        cos = [None, None]
-        sin = [None, None]
+        factor = {}
         rotated = []
         for q in range(Q):
             t, g = divmod(q, G)
-            own = work.tile([P, HALVES, N], F32, name="own")
-            partner = work.tile([P, HALVES, N], F32, name="partner")
+            term = work.tile([P, HALVES, HALVES, N], F32, name="term")
             for h in range(HALVES):
                 window = held.tile([P, S], F32, name=f"emb{h}{q}")
                 nc.sync.dma_start(window[:], emb_windows[h, q])
-                if g == 0:
-                    cos[h] = held.tile([P, G, N], F32, name=f"cos{h}{t}")
-                    nc.sync.dma_start(cos[h][:], cos_pieces[h, t])
-                    sin[1 - h] = held.tile([P, G, N], F32, name=f"sin{1 - h}{t}")
-                    nc.sync.dma_start(sin[1 - h][:], sin_pieces[1 - h, t])
-                looked_up = window[:].indirect(offsets[:])
-                nc.vector.tensor_tensor(own[:, h, :], looked_up, cos[h][:, g, :], MULT)
-                nc.vector.tensor_tensor(partner[:, 1 - h, :], looked_up, sin[1 - h][:, g, :], MULT)
+                for o in range(HALVES):
+                    if g == 0:
+                        pieces = cos_pieces if o == h else sin_pieces
+                        factor[h, o] = held.tile([P, G, N], F32, name=f"factor{h}{o}{t}")
+                        nc.sync.dma_start(factor[h, o][:], pieces[o, t])
+                    nc.vector.tensor_tensor(
+                        term[:, h, o, :], window[:].indirect(offsets[:]), factor[h, o][:, g, :], MULT
+                    )
 
             rotated.append(held.tile([P, HALVES, N], F32, name=f"rotated{q}"))
-            nc.vector.tensor_tensor(rotated[q][:, 0, :], own[:, 0, :], partner[:, 0, :], SUBTRACT)
-            nc.vector.tensor_tensor(rotated[q][:, 1, :], own[:, 1, :], partner[:, 1, :], ADD)
+            nc.vector.tensor_tensor(rotated[q][:, 0, :], term[:, 0, 0, :], term[:, 1, 0, :], SUBTRACT)
+            nc.vector.tensor_tensor(rotated[q][:, 1, :], term[:, 1, 1, :], term[:, 0, 1, :], ADD)
 
         for q in range(Q):
             nc.sync.dma_start(out_pairs[q], rotated[q][:])

@@ -10,40 +10,39 @@ P = 128
 C, S, N = 1024, 512, 128
 HALVES = 2
 Q = C // (HALVES * P)
-G = 2
+G = 4
 
 
 def tile_sedd4rec_kernel(tc, emb, cos_tab, sin_tab, offs, out):
     nc = tc.nc
     emb_windows = emb.rearrange("(h p q) s -> h q p s", h=HALVES, q=Q)
-    cos_pieces = cos_tab.rearrange("(o p t g) n -> o t p g n", o=HALVES, t=Q // G, g=G)
-    sin_pieces = sin_tab.rearrange("(o p t g) n -> o t p g n", o=HALVES, t=Q // G, g=G)
-    out_pairs = out.rearrange("(o p q) n -> q p o n", o=HALVES, q=Q)
+    cos_pieces = cos_tab.rearrange("(h p t g) n -> h t p g n", h=HALVES, t=Q // G, g=G)
+    sin_pieces = sin_tab.rearrange("(h p t g) n -> h t p g n", h=HALVES, t=Q // G, g=G)
+    out_pairs = out.rearrange("(h p q) n -> q p h n", h=HALVES, q=Q)
 
     with tc.tile_pool(name="held", bufs=1) as held, tc.tile_pool(name="work", bufs=3) as work:
         offsets = held.tile([P, N // 16], U16, name="offsets")
         nc.sync.dma_start(offsets[:], offs)
 
-        factor = {}
-        rotated = []
+        cos = [None, None]
+        sin = [None, None]
         for q in range(Q):
             t, g = divmod(q, G)
-            term = work.tile([P, HALVES, HALVES, N], F32, name="term")
+            own = work.tile([P, HALVES, N], F32, name="own")
+            partner = work.tile([P, HALVES, N], F32, name="partner")
             for h in range(HALVES):
                 window = held.tile([P, S], F32, name=f"emb{h}{q}")
                 nc.sync.dma_start(window[:], emb_windows[h, q])
-                for o in range(HALVES):
-                    if g == 0:
-                        pieces = cos_pieces if o == h else sin_pieces
-                        factor[h, o] = held.tile([P, G, N], F32, name=f"factor{h}{o}{t}")
-                        nc.sync.dma_start(factor[h, o][:], pieces[o, t])
-                    nc.vector.tensor_tensor(
-                        term[:, h, o, :], window[:].indirect(offsets[:]), factor[h, o][:, g, :], MULT
-                    )
+                if g == 0:
+                    cos[h] = held.tile([P, G, N], F32, name=f"cos{h}{t}")
+                    nc.sync.dma_start(cos[h][:], cos_pieces[h, t])
+                    sin[1 - h] = held.tile([P, G, N], F32, name=f"sin{1 - h}{t}")
+                    nc.sync.dma_start(sin[1 - h][:], sin_pieces[1 - h, t])
+                looked_up = window[:].indirect(offsets[:])
+                nc.vector.tensor_tensor(own[:, h, :], looked_up, cos[h][:, g, :], MULT)
+                nc.vector.tensor_tensor(partner[:, 1 - h, :], looked_up, sin[1 - h][:, g, :], MULT)
 
-            rotated.append(held.tile([P, HALVES, N], F32, name=f"rotated{q}"))
-            nc.vector.tensor_tensor(rotated[q][:, 0, :], term[:, 0, 0, :], term[:, 1, 0, :], SUBTRACT)
-            nc.vector.tensor_tensor(rotated[q][:, 1, :], term[:, 1, 1, :], term[:, 0, 1, :], ADD)
-
-        for q in range(Q):
-            nc.sync.dma_start(out_pairs[q], rotated[q][:])
+            rotated = work.tile([P, HALVES, N], F32, name="rotated")
+            nc.vector.tensor_tensor(rotated[:, 0, :], own[:, 0, :], partner[:, 0, :], SUBTRACT)
+            nc.vector.tensor_tensor(rotated[:, 1, :], own[:, 1, :], partner[:, 1, :], ADD)
+            nc.scalar.dma_start(out_pairs[q], rotated[:])

@@ -10,7 +10,7 @@ P = 128
 C, S, N = 1024, 512, 128
 HALVES = 2
 Q = C // (HALVES * P)
-G = 4
+G = 2
 
 
 def tile_sedd4rec_kernel(tc, emb, cos_tab, sin_tab, offs, out):
@@ -19,30 +19,38 @@ def tile_sedd4rec_kernel(tc, emb, cos_tab, sin_tab, offs, out):
     cos_pieces = cos_tab.rearrange("(h p t g) n -> h t p g n", h=HALVES, t=Q // G, g=G)
     sin_pieces = sin_tab.rearrange("(h p t g) n -> h t p g n", h=HALVES, t=Q // G, g=G)
     out_pairs = out.rearrange("(h p q) n -> q p h n", h=HALVES, q=Q)
+    queues = (nc.sync, nc.scalar)
 
     with tc.tile_pool(name="held", bufs=1) as held, tc.tile_pool(name="work", bufs=3) as work:
         offsets = held.tile([P, N // 16], U16, name="offsets")
         nc.sync.dma_start(offsets[:], offs)
 
+        loaded = []
+
+        def load(name, shape, source):
+            loaded.append(held.tile(shape, F32, name=name))
+            queues[len(loaded) % 2].dma_start(loaded[-1][:], source)
+            return loaded[-1]
+
         cos = [None, None]
         sin = [None, None]
+        rotated = []
         for q in range(Q):
             t, g = divmod(q, G)
             own = work.tile([P, HALVES, N], F32, name="own")
             partner = work.tile([P, HALVES, N], F32, name="partner")
             for h in range(HALVES):
-                window = held.tile([P, S], F32, name=f"emb{h}{q}")
-                nc.sync.dma_start(window[:], emb_windows[h, q])
+                window = load(f"emb{h}{q}", [P, S], emb_windows[h, q])
                 if g == 0:
-                    cos[h] = held.tile([P, G, N], F32, name=f"cos{h}{t}")
-                    nc.sync.dma_start(cos[h][:], cos_pieces[h, t])
-                    sin[1 - h] = held.tile([P, G, N], F32, name=f"sin{1 - h}{t}")
-                    nc.sync.dma_start(sin[1 - h][:], sin_pieces[1 - h, t])
+                    cos[h] = load(f"cos{h}{t}", [P, G, N], cos_pieces[h, t])
+                    sin[1 - h] = load(f"sin{1 - h}{t}", [P, G, N], sin_pieces[1 - h, t])
                 looked_up = window[:].indirect(offsets[:])
                 nc.vector.tensor_tensor(own[:, h, :], looked_up, cos[h][:, g, :], MULT)
                 nc.vector.tensor_tensor(partner[:, 1 - h, :], looked_up, sin[1 - h][:, g, :], MULT)
 
-            rotated = work.tile([P, HALVES, N], F32, name="rotated")
-            nc.vector.tensor_tensor(rotated[:, 0, :], own[:, 0, :], partner[:, 0, :], SUBTRACT)
-            nc.vector.tensor_tensor(rotated[:, 1, :], own[:, 1, :], partner[:, 1, :], ADD)
-            nc.scalar.dma_start(out_pairs[q], rotated[:])
+            rotated.append(held.tile([P, HALVES, N], F32, name=f"rotated{q}"))
+            nc.vector.tensor_tensor(rotated[q][:, 0, :], own[:, 0, :], partner[:, 0, :], SUBTRACT)
+            nc.vector.tensor_tensor(rotated[q][:, 1, :], own[:, 1, :], partner[:, 1, :], ADD)
+
+        for q in range(Q):
+            queues[q % 2].dma_start(out_pairs[q], rotated[q][:])

@@ -9,19 +9,19 @@ SUBTRACT = mybir.AluOpType.subtract
 P = 128
 C, S, N = 1024, 512, 128
 HALVES = 2
-Q = C // (HALVES * P)
 G = 2
+GROUPS = C // (HALVES * P * G)
 
 
 def tile_sedd4rec_kernel(tc, emb, cos_tab, sin_tab, offs, out):
     nc = tc.nc
-    emb_windows = emb.rearrange("(h p q) s -> h q p s", h=HALVES, q=Q)
-    cos_pieces = cos_tab.rearrange("(h p t g) n -> h t p g n", h=HALVES, t=Q // G, g=G)
-    sin_pieces = sin_tab.rearrange("(h p t g) n -> h t p g n", h=HALVES, t=Q // G, g=G)
-    out_pairs = out.rearrange("(h p q) n -> q p h n", h=HALVES, q=Q)
+    emb_windows = emb.rearrange("(h p t g) s -> h t g p s", h=HALVES, t=GROUPS, g=G)
+    cos_pieces = cos_tab.rearrange("(h p t g) n -> h t p g n", h=HALVES, t=GROUPS, g=G)
+    sin_pieces = sin_tab.rearrange("(h p t g) n -> h t p g n", h=HALVES, t=GROUPS, g=G)
+    out_pieces = out.rearrange("(h p t g) n -> h t p g n", h=HALVES, t=GROUPS, g=G)
     queues = (nc.sync, nc.scalar)
 
-    with tc.tile_pool(name="held", bufs=1) as held, tc.tile_pool(name="work", bufs=3) as work:
+    with tc.tile_pool(name="held", bufs=1) as held, tc.tile_pool(name="work", bufs=2) as work:
         offsets = held.tile([P, N // 16], U16, name="offsets")
         nc.sync.dma_start(offsets[:], offs)
 
@@ -34,23 +34,24 @@ def tile_sedd4rec_kernel(tc, emb, cos_tab, sin_tab, offs, out):
 
         cos = [None, None]
         sin = [None, None]
-        rotated = []
-        for q in range(Q):
-            t, g = divmod(q, G)
-            own = work.tile([P, HALVES, N], F32, name="own")
-            partner = work.tile([P, HALVES, N], F32, name="partner")
+        rotated = {}
+        for t in range(GROUPS):
+            own = work.tile([P, HALVES, G, N], F32, name="own")
+            partner = work.tile([P, HALVES, G, N], F32, name="partner")
+            for g in range(G):
+                for h in range(HALVES):
+                    window = load(f"emb{h}{t}{g}", [P, S], emb_windows[h, t, g])
+                    if g == 0:
+                        cos[h] = load(f"cos{h}{t}", [P, G, N], cos_pieces[h, t])
+                        sin[1 - h] = load(f"sin{1 - h}{t}", [P, G, N], sin_pieces[1 - h, t])
+                    looked_up = window[:].indirect(offsets[:])
+                    nc.vector.tensor_tensor(own[:, h, g, :], looked_up, cos[h][:, g, :], MULT)
+                    nc.vector.tensor_tensor(partner[:, 1 - h, g, :], looked_up, sin[1 - h][:, g, :], MULT)
+
+            for h, join in ((0, SUBTRACT), (1, ADD)):
+                rotated[h, t] = held.tile([P, G, N], F32, name=f"rotated{h}{t}")
+                nc.vector.tensor_tensor(rotated[h, t][:], own[:, h, :, :], partner[:, h, :, :], join)
+
+        for t in range(GROUPS):
             for h in range(HALVES):
-                window = load(f"emb{h}{q}", [P, S], emb_windows[h, q])
-                if g == 0:
-                    cos[h] = load(f"cos{h}{t}", [P, G, N], cos_pieces[h, t])
-                    sin[1 - h] = load(f"sin{1 - h}{t}", [P, G, N], sin_pieces[1 - h, t])
-                looked_up = window[:].indirect(offsets[:])
-                nc.vector.tensor_tensor(own[:, h, :], looked_up, cos[h][:, g, :], MULT)
-                nc.vector.tensor_tensor(partner[:, 1 - h, :], looked_up, sin[1 - h][:, g, :], MULT)
-
-            rotated.append(held.tile([P, HALVES, N], F32, name=f"rotated{q}"))
-            nc.vector.tensor_tensor(rotated[q][:, 0, :], own[:, 0, :], partner[:, 0, :], SUBTRACT)
-            nc.vector.tensor_tensor(rotated[q][:, 1, :], own[:, 1, :], partner[:, 1, :], ADD)
-
-        for q in range(Q):
-            queues[q % 2].dma_start(out_pairs[q], rotated[q][:])
+                queues[h].dma_start(out_pieces[h, t], rotated[h, t][:])

@@ -1,4 +1,5 @@
 import concourse.mybir as mybir
+from concourse.masks import make_identity
 
 F32 = mybir.dt.float32
 U16 = mybir.dt.uint16
@@ -11,6 +12,7 @@ C, S, N = 1024, 512, 128
 HALVES = 2
 G = 2
 GROUPS = C // (HALVES * P * G)
+FLOPS = 3 * C * N
 
 
 def tile_sedd4rec_kernel(tc, emb, cos_tab, sin_tab, offs, out):
@@ -21,9 +23,28 @@ def tile_sedd4rec_kernel(tc, emb, cos_tab, sin_tab, offs, out):
     out_pieces = out.rearrange("(h p t g) n -> h t p g n", h=HALVES, t=GROUPS, g=G)
     queues = (nc.sync, nc.scalar)
 
-    with tc.tile_pool(name="held", bufs=1) as held, tc.tile_pool(name="work", bufs=2) as work:
+    with (
+        tc.tile_pool(name="held", bufs=1) as held,
+        tc.tile_pool(name="work", bufs=2) as work,
+        tc.psum_pool(name="sums", bufs=1) as sums,
+    ):
         offsets = held.tile([P, N // 16], U16, name="offsets")
         nc.sync.dma_start(offsets[:], offs)
+
+        plus = held.tile([P, P], F32, name="plus")
+        minus = held.tile([P, P], F32, name="minus")
+        make_identity(nc, plus[:])
+        nc.gpsimd.memset(minus[:], 0.0)
+        nc.gpsimd.affine_select(
+            out=minus[:],
+            in_=minus[:],
+            compare_op=mybir.AluOpType.not_equal,
+            fill=-1.0,
+            base=0,
+            pattern=[[-1, P]],
+            channel_multiplier=1,
+        )
+        sign = (minus, plus)
 
         loaded = []
 
@@ -38,7 +59,11 @@ def tile_sedd4rec_kernel(tc, emb, cos_tab, sin_tab, offs, out):
         for t in range(GROUPS):
             own = work.tile([P, HALVES, G, N], F32, name="own")
             partner = work.tile([P, HALVES, G, N], F32, name="partner")
+            for h in range(HALVES):
+                rotated[h, t] = held.tile([P, G, N], F32, name=f"rotated{h}{t}")
             for g in range(G):
+                last_pair = (t, g) == (GROUPS - 1, G - 1)
+                total = [None if last_pair else sums.tile([P, N], F32, name=f"total{h}{t}{g}") for h in range(HALVES)]
                 for h in range(HALVES):
                     window = load(f"emb{h}{t}{g}", [P, S], emb_windows[h, t, g])
                     if g == 0:
@@ -47,10 +72,18 @@ def tile_sedd4rec_kernel(tc, emb, cos_tab, sin_tab, offs, out):
                     looked_up = window[:].indirect(offsets[:])
                     nc.vector.tensor_tensor(own[:, h, g, :], looked_up, cos[h][:, g, :], MULT)
                     nc.vector.tensor_tensor(partner[:, 1 - h, g, :], looked_up, sin[1 - h][:, g, :], MULT)
+                    if not last_pair:
+                        opens = h == 0
+                        nc.tensor.matmul(total[h][:], plus[:], own[:, h, g, :], start=opens, stop=not opens)
+                        nc.tensor.matmul(
+                            total[1 - h][:], sign[1 - h][:], partner[:, 1 - h, g, :], start=opens, stop=not opens
+                        )
 
-            for h, join in ((0, SUBTRACT), (1, ADD)):
-                rotated[h, t] = held.tile([P, G, N], F32, name=f"rotated{h}{t}")
-                nc.vector.tensor_tensor(rotated[h, t][:], own[:, h, :, :], partner[:, h, :, :], join)
+                for h, join in ((0, SUBTRACT), (1, ADD)):
+                    if last_pair:
+                        nc.vector.tensor_tensor(rotated[h, t][:, g, :], own[:, h, g, :], partner[:, h, g, :], join)
+                    else:
+                        nc.scalar.copy(rotated[h, t][:, g, :], total[h][:])
 
         for t in range(GROUPS):
             for h in range(HALVES):

@@ -10,24 +10,21 @@ SUBTRACT = mybir.AluOpType.subtract
 P = 128
 C, S, N = 1024, 512, 128
 HALVES = 2
+LOWER, UPPER = 0, 1
+Q = C // (HALVES * P)
 G = 2
-GROUPS = C // (HALVES * P * G)
 FLOPS = 3 * C * N
 
 
 def tile_sedd4rec_kernel(tc, emb, cos_tab, sin_tab, offs, out):
     nc = tc.nc
-    emb_windows = emb.rearrange("(h p t g) s -> h t g p s", h=HALVES, t=GROUPS, g=G)
-    cos_pieces = cos_tab.rearrange("(h p t g) n -> h t p g n", h=HALVES, t=GROUPS, g=G)
-    sin_pieces = sin_tab.rearrange("(h p t g) n -> h t p g n", h=HALVES, t=GROUPS, g=G)
-    out_pieces = out.rearrange("(h p t g) n -> h t p g n", h=HALVES, t=GROUPS, g=G)
+    emb_windows = emb.rearrange("(h p q) s -> h q p s", h=HALVES, q=Q)
+    cos_halves = cos_tab.rearrange("(h p q) n -> h p q n", h=HALVES, q=Q)
+    sin_halves = sin_tab.rearrange("(h p q) n -> h p q n", h=HALVES, q=Q)
+    out_pieces = out.rearrange("(h p t g) n -> h t p g n", h=HALVES, t=Q // G, g=G)
     queues = (nc.sync, nc.scalar)
 
-    with (
-        tc.tile_pool(name="held", bufs=1) as held,
-        tc.tile_pool(name="work", bufs=2) as work,
-        tc.psum_pool(name="sums", bufs=1) as sums,
-    ):
+    with tc.tile_pool(name="held", bufs=1) as held, tc.psum_pool(name="sums", bufs=1) as sums:
         offsets = held.tile([P, N // 16], U16, name="offsets")
         nc.sync.dma_start(offsets[:], offs)
 
@@ -47,44 +44,65 @@ def tile_sedd4rec_kernel(tc, emb, cos_tab, sin_tab, offs, out):
         sign = (minus, plus)
 
         loaded = []
+        shared = 2 * HALVES + 2 * HALVES
 
         def load(name, shape, source):
             loaded.append(held.tile(shape, F32, name=name))
-            queues[len(loaded) % 2].dma_start(loaded[-1][:], source)
+            queue = queues[len(loaded) % 2] if len(loaded) <= shared else nc.sync
+            queue.dma_start(loaded[-1][:], source)
             return loaded[-1]
 
-        cos = [None, None]
-        sin = [None, None]
+        cos = {}
+        sin = {}
+        own = {}
+        partner = {}
+        total = {}
         rotated = {}
-        for t in range(GROUPS):
-            own = work.tile([P, HALVES, G, N], F32, name="own")
-            partner = work.tile([P, HALVES, G, N], F32, name="partner")
+        for t in range(Q // G):
             for h in range(HALVES):
                 rotated[h, t] = held.tile([P, G, N], F32, name=f"rotated{h}{t}")
-            for g in range(G):
-                last_pair = (t, g) == (GROUPS - 1, G - 1)
-                total = [None if last_pair else sums.tile([P, N], F32, name=f"total{h}{t}{g}") for h in range(HALVES)]
-                for h in range(HALVES):
-                    window = load(f"emb{h}{t}{g}", [P, S], emb_windows[h, t, g])
-                    if g == 0:
-                        cos[h] = load(f"cos{h}{t}", [P, G, N], cos_pieces[h, t])
-                        sin[1 - h] = load(f"sin{1 - h}{t}", [P, G, N], sin_pieces[1 - h, t])
-                    looked_up = window[:].indirect(offsets[:])
-                    nc.vector.tensor_tensor(own[:, h, g, :], looked_up, cos[h][:, g, :], MULT)
-                    nc.vector.tensor_tensor(partner[:, 1 - h, g, :], looked_up, sin[1 - h][:, g, :], MULT)
-                    if not last_pair:
-                        opens = h == 0
-                        nc.tensor.matmul(total[h][:], plus[:], own[:, h, g, :], start=opens, stop=not opens)
-                        nc.tensor.matmul(
-                            total[1 - h][:], sign[1 - h][:], partner[:, 1 - h, g, :], start=opens, stop=not opens
-                        )
+        for q in range(Q):
+            own[q] = held.tile([P, HALVES, N], F32, name=f"own{q}")
+            partner[q] = held.tile([P, HALVES, N], F32, name=f"partner{q}")
+        last_pair = Q - 1
 
-                for h, join in ((0, SUBTRACT), (1, ADD)):
-                    if last_pair:
-                        nc.vector.tensor_tensor(rotated[h, t][:, g, :], own[:, h, g, :], partner[:, h, g, :], join)
-                    else:
-                        nc.scalar.copy(rotated[h, t][:, g, :], total[h][:])
+        def look_up(h, q):
+            window = load(f"emb{h}{q}", [P, S], emb_windows[h, q])
+            if q == 0:
+                cos[h] = load(f"cos{h}", [P, Q, N], cos_halves[h])
+                sin[1 - h] = load(f"sin{1 - h}", [P, Q, N], sin_halves[1 - h])
+            looked_up = window[:].indirect(offsets[:])
+            nc.vector.tensor_tensor(own[q][:, h, :], looked_up, cos[h][:, q, :], MULT)
+            nc.vector.tensor_tensor(partner[q][:, 1 - h, :], looked_up, sin[1 - h][:, q, :], MULT)
+            if q != last_pair:
+                opens = h == LOWER
+                if opens:
+                    for half in range(HALVES):
+                        total[half, q] = sums.tile([P, N], F32, name=f"total{half}{q}")
+                nc.tensor.matmul(total[h, q][:], plus[:], own[q][:, h, :], start=opens, stop=not opens)
+                nc.tensor.matmul(
+                    total[1 - h, q][:], sign[1 - h][:], partner[q][:, 1 - h, :], start=opens, stop=not opens
+                )
 
-        for t in range(GROUPS):
+        def finish(q):
+            for h, join in ((LOWER, SUBTRACT), (UPPER, ADD)):
+                piece = rotated[h, q // G][:, q % G, :]
+                if q == last_pair:
+                    nc.vector.tensor_tensor(piece, own[q][:, h, :], partner[q][:, h, :], join)
+                else:
+                    nc.scalar.copy(piece, total[h, q][:])
+
+        look_up(LOWER, 0)
+        look_up(LOWER, 1)
+        look_up(UPPER, 0)
+        finish(0)
+        look_up(UPPER, 1)
+        finish(1)
+        for q in range(2, Q):
+            look_up(LOWER, q)
+            look_up(UPPER, q)
+            finish(q)
+
+        for t in range(Q // G):
             for h in range(HALVES):
                 queues[h].dma_start(out_pieces[h, t], rotated[h, t][:])

@@ -85,7 +85,7 @@ def tile_sedd4rec_kernel(tc, emb, cos_tab, sin_tab, offs, out):
                 )
 
         def finish(q):
-            for h, join in ((LOWER, SUBTRACT), (UPPER, ADD)):
+            for h, join in ((UPPER, ADD), (LOWER, SUBTRACT)):
                 piece = rotated[h, q // G][:, q % G, :]
                 if q == last_pair:
                     nc.vector.tensor_tensor(piece, own[q][:, h, :], partner[q][:, h, :], join)

@@ -18,10 +18,10 @@ FLOPS = 3 * C * N
 
 def tile_sedd4rec_kernel(tc, emb, cos_tab, sin_tab, offs, out):
     nc = tc.nc
-    emb_windows = emb.rearrange("(h p q) s -> h q p s", h=HALVES, q=Q)
-    cos_halves = cos_tab.rearrange("(h p q) n -> h p q n", h=HALVES, q=Q)
-    sin_halves = sin_tab.rearrange("(h p q) n -> h p q n", h=HALVES, q=Q)
-    out_pieces = out.rearrange("(h p t g) n -> h t p g n", h=HALVES, t=Q // G, g=G)
+    emb_windows = emb.rearrange("(h t p g) s -> h t g p s", h=HALVES, t=Q // G, g=G)
+    cos_pieces = cos_tab.rearrange("(h t p g) n -> h t p g n", h=HALVES, t=Q // G, g=G)
+    sin_pieces = sin_tab.rearrange("(h t p g) n -> h t p g n", h=HALVES, t=Q // G, g=G)
+    out_pieces = out.rearrange("(h t p g) n -> h t p g n", h=HALVES, t=Q // G, g=G)
     queues = (nc.sync, nc.scalar)
 
     with tc.tile_pool(name="held", bufs=1) as held, tc.psum_pool(name="sums", bufs=1) as sums:
@@ -44,7 +44,7 @@ def tile_sedd4rec_kernel(tc, emb, cos_tab, sin_tab, offs, out):
         sign = (minus, plus)
 
         loaded = []
-        shared = 2 * HALVES + 2 * HALVES
+        shared = G * HALVES + 2 * HALVES
 
         def load(name, shape, source):
             loaded.append(held.tile(shape, F32, name=name))
@@ -67,13 +67,14 @@ def tile_sedd4rec_kernel(tc, emb, cos_tab, sin_tab, offs, out):
         last_pair = Q - 1
 
         def look_up(h, q):
-            window = load(f"emb{h}{q}", [P, S], emb_windows[h, q])
-            if q == 0:
-                cos[h] = load(f"cos{h}", [P, Q, N], cos_halves[h])
-                sin[1 - h] = load(f"sin{1 - h}", [P, Q, N], sin_halves[1 - h])
+            t, g = q // G, q % G
+            window = load(f"emb{h}{q}", [P, S], emb_windows[h, t, g])
+            if g == 0:
+                cos[h, t] = load(f"cos{h}{t}", [P, G, N], cos_pieces[h, t])
+                sin[1 - h, t] = load(f"sin{1 - h}{t}", [P, G, N], sin_pieces[1 - h, t])
             looked_up = window[:].indirect(offsets[:])
-            nc.vector.tensor_tensor(own[q][:, h, :], looked_up, cos[h][:, q, :], MULT)
-            nc.vector.tensor_tensor(partner[q][:, 1 - h, :], looked_up, sin[1 - h][:, q, :], MULT)
+            nc.vector.tensor_tensor(own[q][:, h, :], looked_up, cos[h, t][:, g, :], MULT)
+            nc.vector.tensor_tensor(partner[q][:, 1 - h, :], looked_up, sin[1 - h, t][:, g, :], MULT)
             if q != last_pair:
                 opens = h == LOWER
                 if opens:
@@ -92,13 +93,7 @@ def tile_sedd4rec_kernel(tc, emb, cos_tab, sin_tab, offs, out):
                 else:
                     nc.scalar.copy(piece, total[h, q][:])
 
-        look_up(LOWER, 0)
-        look_up(LOWER, 1)
-        look_up(UPPER, 0)
-        finish(0)
-        look_up(UPPER, 1)
-        finish(1)
-        for q in range(2, Q):
+        for q in range(Q):
             look_up(LOWER, q)
             look_up(UPPER, q)
             finish(q)

@@ -18,10 +18,10 @@ FLOPS = 3 * C * N
 
 def tile_sedd4rec_kernel(tc, emb, cos_tab, sin_tab, offs, out):
     nc = tc.nc
-    emb_windows = emb.rearrange("(h t p g) s -> h t g p s", h=HALVES, t=Q // G, g=G)
-    cos_pieces = cos_tab.rearrange("(h t p g) n -> h t p g n", h=HALVES, t=Q // G, g=G)
-    sin_pieces = sin_tab.rearrange("(h t p g) n -> h t p g n", h=HALVES, t=Q // G, g=G)
-    out_pieces = out.rearrange("(h t p g) n -> h t p g n", h=HALVES, t=Q // G, g=G)
+    emb_windows = emb.rearrange("(h p t g) s -> h t g p s", h=HALVES, t=Q // G, g=G)
+    cos_pieces = cos_tab.rearrange("(h p t g) n -> h t p g n", h=HALVES, t=Q // G, g=G)
+    sin_pieces = sin_tab.rearrange("(h p t g) n -> h t p g n", h=HALVES, t=Q // G, g=G)
+    out_halves = out.rearrange("(h p q) n -> h p q n", h=HALVES, q=Q)
     queues = (nc.sync, nc.scalar)
 
     with tc.tile_pool(name="held", bufs=1) as held, tc.psum_pool(name="sums", bufs=1) as sums:
@@ -57,14 +57,15 @@ def tile_sedd4rec_kernel(tc, emb, cos_tab, sin_tab, offs, out):
         own = {}
         partner = {}
         total = {}
+        last_pair = Q - 1
+        summed = {}
         rotated = {}
-        for t in range(Q // G):
-            for h in range(HALVES):
-                rotated[h, t] = held.tile([P, G, N], F32, name=f"rotated{h}{t}")
+        for h in range(HALVES):
+            summed[h] = held.tile([P, last_pair, N], F32, name=f"summed{h}")
+            rotated[h] = held.tile([P, N], F32, name=f"rotated{h}")
         for q in range(Q):
             own[q] = held.tile([P, HALVES, N], F32, name=f"own{q}")
             partner[q] = held.tile([P, HALVES, N], F32, name=f"partner{q}")
-        last_pair = Q - 1
 
         def look_up(h, q):
             t, g = q // G, q % G
@@ -87,17 +88,17 @@ def tile_sedd4rec_kernel(tc, emb, cos_tab, sin_tab, offs, out):
 
         def finish(q):
             for h, join in ((UPPER, ADD), (LOWER, SUBTRACT)):
-                piece = rotated[h, q // G][:, q % G, :]
                 if q == last_pair:
-                    nc.vector.tensor_tensor(piece, own[q][:, h, :], partner[q][:, h, :], join)
+                    nc.vector.tensor_tensor(rotated[h][:], own[q][:, h, :], partner[q][:, h, :], join)
                 else:
-                    nc.scalar.copy(piece, total[h, q][:])
+                    nc.scalar.copy(summed[h][:, q, :], total[h, q][:])
 
         for q in range(Q):
             look_up(LOWER, q)
             look_up(UPPER, q)
             finish(q)
 
-        for t in range(Q // G):
-            for h in range(HALVES):
-                queues[h].dma_start(out_pieces[h, t], rotated[h, t][:])
+        for h in (UPPER, LOWER):
+            nc.scalar.dma_start(out_halves[h][:, :last_pair, :], summed[h][:])
+        for h in (UPPER, LOWER):
+            nc.sync.dma_start(out_halves[h][:, last_pair, :], rotated[h][:])

@@ -18,11 +18,10 @@ FLOPS = 3 * C * N
 
 def tile_sedd4rec_kernel(tc, emb, cos_tab, sin_tab, offs, out):
     nc = tc.nc
-    emb_windows = emb.rearrange("(h p t g) s -> h t g p s", h=HALVES, t=Q // G, g=G)
-    cos_pieces = cos_tab.rearrange("(h p t g) n -> h t p g n", h=HALVES, t=Q // G, g=G)
-    sin_pieces = sin_tab.rearrange("(h p t g) n -> h t p g n", h=HALVES, t=Q // G, g=G)
+    emb_windows = emb.rearrange("(h p q) s -> h q p s", h=HALVES, q=Q)
+    cos_halves = cos_tab.rearrange("(h p q) n -> h p q n", h=HALVES, q=Q)
+    sin_halves = sin_tab.rearrange("(h p q) n -> h p q n", h=HALVES, q=Q)
     out_halves = out.rearrange("(h p q) n -> h p q n", h=HALVES, q=Q)
-    queues = (nc.sync, nc.scalar)
 
     with tc.tile_pool(name="held", bufs=1) as held, tc.psum_pool(name="sums", bufs=1) as sums:
         offsets = held.tile([P, N // 16], U16, name="offsets")
@@ -43,17 +42,38 @@ def tile_sedd4rec_kernel(tc, emb, cos_tab, sin_tab, offs, out):
         )
         sign = (minus, plus)
 
-        loaded = []
-        shared = G * HALVES + 2 * HALVES
+        def load(queue, name, shape, source):
+            tile = held.tile(shape, F32, name=name)
+            queue.dma_start(tile[:], source)
+            return tile
 
-        def load(name, shape, source):
-            loaded.append(held.tile(shape, F32, name=name))
-            queue = queues[len(loaded) % 2] if len(loaded) <= shared else nc.sync
-            queue.dma_start(loaded[-1][:], source)
-            return loaded[-1]
-
+        window = {}
         cos = {}
         sin = {}
+
+        def load_window(queue, h, q):
+            window[h, q] = load(queue, f"emb{h}{q}", [P, S], emb_windows[h, q])
+
+        def load_rows(queue, rows, table, h, halves, first, count):
+            piece = load(queue, f"{table}{h}{first}", [P, count, N], halves[h][:, first : first + count, :])
+            for k in range(count):
+                rows[h, first + k] = piece[:, k, :]
+
+        load_window(nc.scalar, LOWER, 0)
+        load_rows(nc.sync, cos, "cos", LOWER, cos_halves, 0, G)
+        load_rows(nc.scalar, sin, "sin", UPPER, sin_halves, 0, Q)
+        load_window(nc.sync, LOWER, 1)
+        load_rows(nc.scalar, cos, "cos", UPPER, cos_halves, 0, Q)
+        load_window(nc.sync, UPPER, 0)
+        load_rows(nc.scalar, sin, "sin", LOWER, sin_halves, 0, G)
+        load_window(nc.sync, UPPER, 1)
+        load_window(nc.sync, LOWER, 2)
+        load_rows(nc.sync, cos, "cos", LOWER, cos_halves, G, Q - G)
+        load_window(nc.sync, UPPER, 2)
+        load_rows(nc.sync, sin, "sin", LOWER, sin_halves, G, Q - G)
+        load_window(nc.sync, LOWER, 3)
+        load_window(nc.sync, UPPER, 3)
+
         own = {}
         partner = {}
         total = {}
@@ -68,14 +88,17 @@ def tile_sedd4rec_kernel(tc, emb, cos_tab, sin_tab, offs, out):
             partner[q] = held.tile([P, HALVES, N], F32, name=f"partner{q}")
 
         def look_up(h, q):
-            t, g = q // G, q % G
-            window = load(f"emb{h}{q}", [P, S], emb_windows[h, t, g])
-            if g == 0:
-                cos[h, t] = load(f"cos{h}{t}", [P, G, N], cos_pieces[h, t])
-                sin[1 - h, t] = load(f"sin{1 - h}{t}", [P, G, N], sin_pieces[1 - h, t])
-            looked_up = window[:].indirect(offsets[:])
-            nc.vector.tensor_tensor(own[q][:, h, :], looked_up, cos[h, t][:, g, :], MULT)
-            nc.vector.tensor_tensor(partner[q][:, 1 - h, :], looked_up, sin[1 - h, t][:, g, :], MULT)
+            looked_up = window[h, q][:].indirect(offsets[:])
+
+            def own_product():
+                nc.vector.tensor_tensor(own[q][:, h, :], looked_up, cos[h, q], MULT)
+
+            def partner_product():
+                nc.vector.tensor_tensor(partner[q][:, 1 - h, :], looked_up, sin[1 - h, q], MULT)
+
+            partner_first = h == LOWER and q >= G
+            for product in (partner_product, own_product) if partner_first else (own_product, partner_product):
+                product()
             if q != last_pair:
                 opens = h == LOWER
                 if opens:
@@ -93,11 +116,15 @@ def tile_sedd4rec_kernel(tc, emb, cos_tab, sin_tab, offs, out):
                 else:
                     nc.scalar.copy(summed[h][:, q, :], total[h, q][:])
 
-        for q in range(Q):
+        for q in range(G):
+            look_up(LOWER, q)
+        for q in range(G):
+            look_up(UPPER, q)
+            finish(q)
+        for q in range(G, Q):
             look_up(LOWER, q)
             look_up(UPPER, q)
             finish(q)
-
         for h in (UPPER, LOWER):
             nc.scalar.dma_start(out_halves[h][:, :last_pair, :], summed[h][:])
         for h in (UPPER, LOWER):

@@ -90,24 +90,20 @@ def tile_sedd4rec_kernel(tc, emb, cos_tab, sin_tab, offs, out):
         def look_up(h, q):
             looked_up = window[h, q][:].indirect(offsets[:])
 
-            def own_product():
-                nc.vector.tensor_tensor(own[q][:, h, :], looked_up, cos[h, q], MULT)
-
-            def partner_product():
-                nc.vector.tensor_tensor(partner[q][:, 1 - h, :], looked_up, sin[1 - h, q], MULT)
-
-            partner_first = h == LOWER and q >= G
-            for product in (partner_product, own_product) if partner_first else (own_product, partner_product):
-                product()
-            if q != last_pair:
-                opens = h == LOWER
-                if opens:
-                    for half in range(HALVES):
+            def multiply(products, half, row, weights):
+                product = products[q][:, half, :]
+                nc.vector.tensor_tensor(product, looked_up, row, MULT)
+                if q != last_pair:
+                    opens = h == LOWER
+                    if opens:
                         total[half, q] = sums.tile([P, N], F32, name=f"total{half}{q}")
-                nc.tensor.matmul(total[h, q][:], plus[:], own[q][:, h, :], start=opens, stop=not opens)
-                nc.tensor.matmul(
-                    total[1 - h, q][:], sign[1 - h][:], partner[q][:, 1 - h, :], start=opens, stop=not opens
-                )
+                    nc.tensor.matmul(total[half, q][:], weights[:], product, start=opens, stop=not opens)
+
+            own_product = (own, h, cos[h, q], plus)
+            partner_product = (partner, 1 - h, sin[1 - h, q], sign[1 - h])
+            partner_first = h == LOWER and q >= G
+            for factors in (partner_product, own_product) if partner_first else (own_product, partner_product):
+                multiply(*factors)
 
         def finish(q):
             for h, join in ((UPPER, ADD), (LOWER, SUBTRACT)):

import concourse.mybir as mybir
from concourse.masks import make_identity

F32 = mybir.dt.float32
U16 = mybir.dt.uint16
MULT = mybir.AluOpType.mult
ADD = mybir.AluOpType.add
SUBTRACT = mybir.AluOpType.subtract

P = 128
C, S, N = 1024, 512, 128
HALVES = 2
LOWER, UPPER = 0, 1
Q = C // (HALVES * P)
G = 2
FLOPS = 3 * C * N


def tile_sedd4rec_kernel(tc, emb, cos_tab, sin_tab, offs, out):
    nc = tc.nc
    emb_windows = emb.rearrange("(h p q) s -> h q p s", h=HALVES, q=Q)
    cos_halves = cos_tab.rearrange("(h p q) n -> h p q n", h=HALVES, q=Q)
    sin_halves = sin_tab.rearrange("(h p q) n -> h p q n", h=HALVES, q=Q)
    out_halves = out.rearrange("(h p q) n -> h p q n", h=HALVES, q=Q)

    with tc.tile_pool(name="held", bufs=1) as held, tc.psum_pool(name="sums", bufs=1) as sums:
        offsets = held.tile([P, N // 16], U16, name="offsets")
        nc.sync.dma_start(offsets[:], offs)

        plus = held.tile([P, P], F32, name="plus")
        minus = held.tile([P, P], F32, name="minus")
        make_identity(nc, plus[:])
        nc.gpsimd.memset(minus[:], 0.0)
        nc.gpsimd.affine_select(
            out=minus[:],
            in_=minus[:],
            compare_op=mybir.AluOpType.not_equal,
            fill=-1.0,
            base=0,
            pattern=[[-1, P]],
            channel_multiplier=1,
        )
        sign = (minus, plus)

        def load(queue, name, shape, source):
            tile = held.tile(shape, F32, name=name)
            queue.dma_start(tile[:], source)
            return tile

        window = {}
        cos = {}
        sin = {}

        def load_window(queue, h, q):
            window[h, q] = load(queue, f"emb{h}{q}", [P, S], emb_windows[h, q])

        def load_rows(queue, rows, table, h, halves, first, count):
            piece = load(queue, f"{table}{h}{first}", [P, count, N], halves[h][:, first : first + count, :])
            for k in range(count):
                rows[h, first + k] = piece[:, k, :]

        load_window(nc.scalar, LOWER, 0)
        load_rows(nc.sync, cos, "cos", LOWER, cos_halves, 0, G)
        load_rows(nc.scalar, sin, "sin", UPPER, sin_halves, 0, Q)
        load_window(nc.sync, LOWER, 1)
        load_rows(nc.scalar, cos, "cos", UPPER, cos_halves, 0, Q)
        load_window(nc.sync, UPPER, 0)
        load_rows(nc.scalar, sin, "sin", LOWER, sin_halves, 0, G)
        load_window(nc.sync, UPPER, 1)
        load_window(nc.sync, LOWER, 2)
        load_rows(nc.sync, cos, "cos", LOWER, cos_halves, G, Q - G)
        load_window(nc.sync, UPPER, 2)
        load_rows(nc.sync, sin, "sin", LOWER, sin_halves, G, Q - G)
        load_window(nc.sync, LOWER, 3)
        load_window(nc.sync, UPPER, 3)

        own = {}
        partner = {}
        total = {}
        last_pair = Q - 1
        summed = {}
        rotated = {}
        for h in range(HALVES):
            summed[h] = held.tile([P, last_pair, N], F32, name=f"summed{h}")
            rotated[h] = held.tile([P, N], F32, name=f"rotated{h}")
        for q in range(Q):
            own[q] = held.tile([P, HALVES, N], F32, name=f"own{q}")
            partner[q] = held.tile([P, HALVES, N], F32, name=f"partner{q}")

        def look_up(h, q):
            looked_up = window[h, q][:].indirect(offsets[:])

            def multiply(products, half, row, weights):
                product = products[q][:, half, :]
                nc.vector.tensor_tensor(product, looked_up, row, MULT)
                if q != last_pair:
                    opens = h == LOWER
                    if opens:
                        total[half, q] = sums.tile([P, N], F32, name=f"total{half}{q}")
                    nc.tensor.matmul(total[half, q][:], weights[:], product, start=opens, stop=not opens)

            own_product = (own, h, cos[h, q], plus)
            partner_product = (partner, 1 - h, sin[1 - h, q], sign[1 - h])
            partner_first = h == LOWER and q >= G
            for factors in (partner_product, own_product) if partner_first else (own_product, partner_product):
                multiply(*factors)

        def finish(q):
            for h, join in ((UPPER, ADD), (LOWER, SUBTRACT)):
                if q == last_pair:
                    nc.vector.tensor_tensor(rotated[h][:], own[q][:, h, :], partner[q][:, h, :], join)
                else:
                    nc.scalar.copy(summed[h][:, q, :], total[h, q][:])

        for q in range(G):
            look_up(LOWER, q)
        for q in range(G):
            look_up(UPPER, q)
            finish(q)
        for q in range(G, Q):
            look_up(LOWER, q)
            look_up(UPPER, q)
            finish(q)
        for h in (UPPER, LOWER):
            nc.scalar.dma_start(out_halves[h][:, :last_pair, :], summed[h][:])
        for h in (UPPER, LOWER):
            nc.sync.dma_start(out_halves[h][:, last_pair, :], rotated[h][:])
